import numpy as np
import ml_dtypes


def mxq(x, axis, fmt="e4m3"):
    dtype, down = {"e4m3": (ml_dtypes.float8_e4m3fn, 7), "e5m2": (ml_dtypes.float8_e5m2, 14)}[fmt]
    v = np.moveaxis(np.asarray(x, np.float32).astype(ml_dtypes.bfloat16).astype(np.float64), axis, -1)
    blocks = v.reshape(v.shape[:-1] + (-1, 32))
    amax = np.abs(blocks).max(-1, keepdims=True)
    byte = np.maximum(np.where(amax > 0, np.frexp(amax)[1] - 1 + 127, 0) - down, 1)
    scale = np.exp2(byte - 127.0)
    codes = (blocks / scale).astype(np.float32).astype(dtype).astype(np.float64)
    return np.moveaxis((codes * scale).reshape(v.shape), -1, axis)


WIDE = False


def mx_kscale(k):
    if not WIDE:
        return np.ones(k)
    levels = np.array([10, -10, 5, -5, 0])
    a = np.random.permutation(np.resize(levels, k // 512 * 4)).reshape(k // 512, 4)
    idx = np.arange(k)
    return np.exp2(a[idx // 512, idx % 128 // 32])


BF16 = ml_dtypes.bfloat16


def bf(x):
    return np.asarray(x, np.float32).astype(BF16)


def f64(x):
    return np.asarray(x).astype(np.float64)


E2M1 = np.array([0.0, 0.5, 1.0, 1.5, 2.0, 3.0, 4.0, 6.0, -0.0, -0.5, -1.0, -1.5, -2.0, -3.0, -4.0, -6.0])


def pack_weight(w, fmt):
    k, n = w.shape
    w = f64(bf(w)).reshape(k // 32, 32, n)
    amax = np.abs(w).max(1)
    if fmt == "e4m3":
        byte = np.frexp(amax)[1] - 1 + 127 - 7
    else:
        mant, ex = np.frexp(amax / 6.0)
        byte = np.where(mant > 0.5, ex, ex - 1) + 127
    byte = np.clip(np.where(amax > 0, byte, 1), 1, 254)
    scaled = (w * np.exp2(127.0 - byte)[:, None, :]).reshape(k, n).astype(np.float32)
    by_word = np.ascontiguousarray(scaled.reshape(k // 512, 128, 4, n).transpose(0, 1, 3, 2))
    if fmt == "e4m3":
        words = by_word.astype(ml_dtypes.float8_e4m3fn).view(np.uint8)
    else:
        c = by_word.astype(ml_dtypes.float4_e2m1fn).view(np.uint8) & 0xF
        words = c[..., 0::2] | (c[..., 1::2] << 4)
    return np.ascontiguousarray(words), np.ascontiguousarray(byte.astype(np.uint8).reshape(k // 512, 16, n))


def unpack_weight(words, scales, fmt):
    g, p, n, _ = words.shape
    if fmt == "e4m3":
        vals = np.ascontiguousarray(words).view(ml_dtypes.float8_e4m3fn).astype(np.float64)
    else:
        nib = np.empty((g, p, n, 4), np.uint8)
        nib[..., 0::2] = words & 0xF
        nib[..., 1::2] = words >> 4
        vals = E2M1[nib]
    vals = vals * np.repeat(np.exp2(scales.astype(np.float64) - 127.0), 8, axis=1)[..., None]
    return vals.transpose(0, 1, 3, 2).reshape(g * 512, n)

def pack4(w):
    words, scales = pack_weight(w, "e2m1")
    return words.reshape(words.shape[0], 128, -1), scales


def unpack4(words, scales):
    return unpack_weight(words.reshape(words.shape[0], 128, -1, 2), scales, "e2m1")


S, B, H, NH, HD, MAX_END = 64, 2, 16384, 16, 64, 4096
THETA = 10000.0
HALF = HD // 2
O = NH * 2 * HD


def rope(x, cos, sin):
    xr = x.reshape(S, B, NH, HALF, 2)
    x0, x1 = xr[..., 0], xr[..., 1]
    c = cos[:, None, None, :]
    sn = sin[:, None, None, :]
    o0 = x0 * c - x1 * sn
    o1 = x0 * sn + x1 * c
    return np.stack([o0, o1], axis=-1).reshape(x.shape)


def setup_inputs():
    s = mx_kscale(H)
    freqs = 1.0 / THETA ** (np.arange(0, HD, 2) / HD)
    ang = np.outer(np.arange(S), freqs)
    hidden_states = bf(np.random.standard_normal((S, B, H)) * s)
    w_qk = np.random.standard_normal((O, H)) / np.sqrt(H) / s
    words, scales = pack4(np.ascontiguousarray(w_qk.T))
    return {"hidden_states": hidden_states,
            "w_qk_words": words,
            "w_qk_scales": scales,
            "cos": bf(np.cos(ang)),
            "sin": bf(np.sin(ang))}


def reference(hidden_states, w_qk_words, w_qk_scales, cos, sin):
    mixed = mxq(f64(hidden_states), 2, "e4m3") @ unpack4(w_qk_words, w_qk_scales)
    mixed = mixed.reshape(S, B, NH, 2 * HD)
    q, k = mixed[..., :HD], mixed[..., HD:]
    q = rope(q, f64(cos), f64(sin))
    k = rope(k, f64(cos), f64(sin))
    qb = q.transpose(1, 2, 0, 3).reshape(B * NH, S, HD)
    kb = k.transpose(1, 2, 0, 3).reshape(B * NH, S, HD)
    return qb, kb

@@ -1,0 +1,190 @@
+from contextlib import ExitStack
+
+import concourse.mybir as mybir
+from concourse.masks import make_identity
+
+F32 = mybir.dt.float32
+BF16 = mybir.dt.bfloat16
+I32 = mybir.dt.int32
+U32 = mybir.dt.uint32
+U8 = mybir.dt.uint8
+FP8X4 = mybir.dt.float8_e4m3fn_x4
+FP4X4 = mybir.dt.float4_e2m1fn_x4
+
+P = 128
+PACK = 4
+K_PASS = P * PACK
+POSITIONS, BATCH, FEATURES = 64, 2, 16384
+TOKENS = POSITIONS * BATCH
+HEADS, HEAD_DIM = 16, 64
+PAIRS = HEAD_DIM // 2
+N_OUT = HEADS * 2 * HEAD_DIM
+N_TILE = 512
+BANKS = N_OUT // N_TILE
+VECTORS = N_TILE // HEAD_DIM
+HEADS_PER_BANK = VECTORS // 2
+GROUPS = FEATURES // K_PASS
+
+STRETCH = 8
+STRETCHES = GROUPS // STRETCH
+SCALE_GROUPS_PER_DMA = 4
+TAPER = 4
+MAIN_GROUPS = GROUPS - TAPER
+W_BUFS = 16
+
+FLOPS = 2 * TOKENS * FEATURES * N_OUT
+
+
+def load_scale_rows(nc, w_planes, w_scales, stretch):
+    for first_group in range(stretch * STRETCH, (stretch + 1) * STRETCH, SCALE_GROUPS_PER_DMA):
+        groups = slice(first_group, first_group + SCALE_GROUPS_PER_DMA)
+        for quadrant in range(2):
+            for row in range(4):
+                nc.sync.dma_start(
+                    out=w_planes[32 * quadrant + row : P : 64, groups, :].bitcast(I32),
+                    in_=w_scales[groups, 4 * quadrant + row : 16 : 8, :].rearrange("g q n -> q g n"),
+                )
+
+
+def tile_repro_pa_k_kernel(tc, hidden_states, w_qk_words, w_qk_scales, cos, sin, out_0, out_1):
+    nc = tc.nc
+    x_rows = hidden_states.rearrange("s b k -> (s b) k")
+    w_words = w_qk_words.bitcast(I32)
+    w_scales = w_qk_scales.bitcast(I32)
+
+    with ExitStack() as stack:
+        stack.enter_context(tc.manual_schedule())
+        keep = stack.enter_context(tc.tile_pool(name="keep", bufs=1))
+        x_pool = stack.enter_context(tc.tile_pool(name="x", bufs=STRETCHES))
+        grouped_pool = stack.enter_context(tc.tile_pool(name="grouped", bufs=2))
+        w_pool = stack.enter_context(tc.tile_pool(name="w", bufs=W_BUFS))
+        tail_pool = stack.enter_context(tc.tile_pool(name="tail", bufs=BANKS))
+        rope_pool = stack.enter_context(tc.tile_pool(name="rope", bufs=2))
+        acc_pool = stack.enter_context(tc.psum_pool(name="acc", bufs=1))
+        xt_pool = stack.enter_context(tc.psum_pool(name="xt", bufs=4))
+
+        identity = keep.tile([P, P], F32)
+        make_identity(nc, identity[:])
+
+        w_planes = keep.tile([P, GROUPS, N_OUT], U8, align_bytes=64)
+        for stretch in range(STRETCHES):
+            groups = slice(stretch * STRETCH, (stretch + 1) * STRETCH)
+            nc.vector.memset(w_planes[:, groups, :].bitcast(I32), 0)
+
+        x_chunks = []
+        for stretch in range(STRETCHES):
+            x_chunk = x_pool.tile([P, STRETCH * K_PASS], BF16)
+            columns = slice(stretch * STRETCH * K_PASS, (stretch + 1) * STRETCH * K_PASS)
+            nc.sync.dma_start(out=x_chunk[:], in_=x_rows[:, columns])
+            x_chunks.append(x_chunk)
+        cos_bf = keep.tile([P, PAIRS], BF16)
+        sin_bf = keep.tile([P, PAIRS], BF16)
+        for b in range(BATCH):
+            nc.sync.dma_start(out=cos_bf[b:P:BATCH, :], in_=cos)
+            nc.sync.dma_start(out=sin_bf[b:P:BATCH, :], in_=sin)
+
+        def load_group(g):
+            if g % STRETCH == 0:
+                load_scale_rows(nc, w_planes, w_scales, g // STRETCH)
+            w_tile = w_pool.tile([P, 2 * N_OUT], U8, align_bytes=64)
+            nc.sync.dma_start(out=w_tile[:].bitcast(I32), in_=w_words[g])
+            return w_tile
+
+        w_tiles = [load_group(g) for g in range(W_BUFS)]
+
+        x_codes = keep.tile([P, GROUPS * TOKENS], U32, align_bytes=64)
+        x_planes = keep.tile([P, GROUPS * TOKENS], U8, align_bytes=64)
+        for stretch in range(STRETCHES):
+            x_words = x_chunks[stretch][:].bitcast(F32)
+            grouped = grouped_pool.tile([P, STRETCH * TOKENS * PACK], BF16, align_bytes=64)
+            grouped_words = grouped[:].bitcast(F32).rearrange("p (g r u) -> p g r u", g=STRETCH, u=2)
+            for bank in range(STRETCH // 2):
+                xt = xt_pool.tile([P, 2, 2, TOKENS], F32)
+                for i in range(2):
+                    g = 2 * bank + i
+                    for u in range(2):
+                        nc.tensor.transpose(
+                            out=xt[:, i, u, :],
+                            in_=x_words[:, 256 * g + u : 256 * (g + 1) : 2],
+                            identity=identity[:],
+                        )
+                copy_out = nc.vector.tensor_copy if bank % 2 == 0 else nc.scalar.copy
+                copy_out(
+                    out=grouped_words[:, 2 * bank : 2 * bank + 2, :, :],
+                    in_=xt[:].rearrange("p g u r -> p g r u"),
+                )
+            columns = slice(stretch * STRETCH * TOKENS, (stretch + 1) * STRETCH * TOKENS)
+            nc.vector.quantize_mx(
+                out=x_codes[:, columns].bitcast(FP8X4),
+                scales=x_planes[:, columns],
+                in_=grouped[:],
+            )
+
+        cos_f = keep.tile([P, PAIRS], F32)
+        sin_signed = keep.tile([P, 2, PAIRS], F32)
+        nc.vector.tensor_copy(out=cos_f[:], in_=cos_bf[:])
+        nc.vector.tensor_scalar_mul(out=sin_signed[:, 0, :], in0=sin_bf[:], scalar1=-1.0)
+        nc.vector.tensor_copy(out=sin_signed[:, 1, :], in_=sin_bf[:])
+
+        acc = [acc_pool.tile([P, N_TILE], F32, name="acc%d" % j) for j in range(BANKS)]
+
+        def one_pass(g, j, w_codes):
+            tokens = slice(g * TOKENS, (g + 1) * TOKENS)
+            nc.tensor.matmul_mx(
+                out=acc[j][:],
+                lhsT=x_codes[:, tokens].bitcast(FP8X4),
+                lhsT_scale=x_planes[:, tokens],
+                rhs=w_codes.bitcast(FP4X4),
+                rhs_scale=w_planes[:, g, j * N_TILE : (j + 1) * N_TILE],
+                start=(g == 0),
+                stop=(g == GROUPS - 1),
+            )
+
+        for g in range(MAIN_GROUPS):
+            for j in range(BANKS):
+                one_pass(g, j, w_tiles[g][:, 2 * j * N_TILE : 2 * (j + 1) * N_TILE])
+            if g + W_BUFS < MAIN_GROUPS:
+                w_tiles.append(load_group(g + W_BUFS))
+
+        tails = []
+        for j in range(BANKS):
+            tail = tail_pool.tile([P, TAPER, 2 * N_TILE], U8, align_bytes=64)
+            nc.sync.dma_start(
+                out=tail[:].bitcast(I32),
+                in_=w_words[MAIN_GROUPS:GROUPS, :, j * N_TILE // 2 : (j + 1) * N_TILE // 2].rearrange("g p c -> p g c"),
+            )
+            tails.append(tail)
+
+        for j in range(BANKS):
+            for i in range(TAPER):
+                one_pass(MAIN_GROUPS + i, j, tails[j][:, i, :])
+
+            x = acc[j][:].rearrange("p (v r e) -> p v r e", r=PAIRS, e=2)
+            by_cos = rope_pool.tile([P, VECTORS, PAIRS, 2], F32)
+            nc.vector.tensor_mul(
+                out=by_cos[:],
+                in0=x,
+                in1=cos_f[:].unsqueeze(1).unsqueeze(3).to_broadcast([P, VECTORS, PAIRS, 2]),
+            )
+            by_sin = rope_pool.tile([P, 2, VECTORS, PAIRS], F32)
+            for e in range(2):
+                nc.vector.tensor_mul(
+                    out=by_sin[:, e, :, :],
+                    in0=x[:, :, :, 1 - e],
+                    in1=sin_signed[:, e, :].unsqueeze(1).to_broadcast([P, VECTORS, PAIRS]),
+                )
+            rotated = rope_pool.tile([P, VECTORS, PAIRS, 2], F32)
+            nc.vector.tensor_add(
+                out=rotated[:],
+                in0=by_cos[:],
+                in1=by_sin[:].rearrange("p e v r -> p v r e"),
+            )
+
+            by_head = rotated[:].rearrange("p (h t) r e -> p h t (r e)", t=2)
+            for t, out_t in enumerate((out_0, out_1)):
+                for b in range(BATCH):
+                    first_head = b * HEADS + j * HEADS_PER_BANK
+                    nc.sync.dma_start(
+                        out=out_t[first_head : first_head + HEADS_PER_BANK].rearrange("h s d -> s h d"),
+                        in_=by_head[b:P:BATCH, :, t, :],
+                    )

@@ -35,13 +35,14 @@ W_BUFS = 16
 FLOPS = 2 * TOKENS * FEATURES * N_OUT
 
 
-def load_scale_rows(nc, w_planes, w_scales, stretch):
-    for first_group in range(stretch * STRETCH, (stretch + 1) * STRETCH, SCALE_GROUPS_PER_DMA):
-        groups = slice(first_group, first_group + SCALE_GROUPS_PER_DMA)
+def load_scale_rows(nc, planes, w_scales, stretch):
+    for first in range(0, STRETCH, SCALE_GROUPS_PER_DMA):
+        local = slice(first, first + SCALE_GROUPS_PER_DMA)
+        groups = slice(stretch * STRETCH + first, stretch * STRETCH + first + SCALE_GROUPS_PER_DMA)
         for quadrant in range(2):
             for row in range(4):
                 nc.sync.dma_start(
-                    out=w_planes[32 * quadrant + row : P : 64, groups, :].bitcast(I32),
+                    out=planes[32 * quadrant + row : P : 64, local, :].bitcast(I32),
                     in_=w_scales[groups, 4 * quadrant + row : 16 : 8, :].rearrange("g q n -> q g n"),
                 )
 
@@ -56,6 +57,8 @@ def tile_repro_pa_k_kernel(tc, hidden_states, w_qk_words, w_qk_scales, cos, sin,
         stack.enter_context(tc.manual_schedule())
         keep = stack.enter_context(tc.tile_pool(name="keep", bufs=1))
         x_pool = stack.enter_context(tc.tile_pool(name="x", bufs=STRETCHES))
+        quantised_pool = stack.enter_context(tc.tile_pool(name="quantised", bufs=STRETCHES))
+        plane_pool = stack.enter_context(tc.tile_pool(name="planes", bufs=STRETCHES))
         grouped_pool = stack.enter_context(tc.tile_pool(name="grouped", bufs=2))
         w_pool = stack.enter_context(tc.tile_pool(name="w", bufs=W_BUFS))
         tail_pool = stack.enter_context(tc.tile_pool(name="tail", bufs=BANKS))
@@ -65,11 +68,6 @@ def tile_repro_pa_k_kernel(tc, hidden_states, w_qk_words, w_qk_scales, cos, sin,
 
         identity = keep.tile([P, P], F32)
         make_identity(nc, identity[:])
-
-        w_planes = keep.tile([P, GROUPS, N_OUT], U8, align_bytes=64)
-        for stretch in range(STRETCHES):
-            groups = slice(stretch * STRETCH, (stretch + 1) * STRETCH)
-            nc.vector.memset(w_planes[:, groups, :].bitcast(I32), 0)
 
         x_chunks = []
         for stretch in range(STRETCHES):
@@ -83,17 +81,22 @@ def tile_repro_pa_k_kernel(tc, hidden_states, w_qk_words, w_qk_scales, cos, sin,
             nc.sync.dma_start(out=cos_bf[b:P:BATCH, :], in_=cos)
             nc.sync.dma_start(out=sin_bf[b:P:BATCH, :], in_=sin)
 
+        w_planes = []
+
         def load_group(g):
             if g % STRETCH == 0:
-                load_scale_rows(nc, w_planes, w_scales, g // STRETCH)
+                planes = plane_pool.tile([P, STRETCH, N_OUT], U8, align_bytes=64)
+                nc.vector.memset(planes[:].bitcast(I32), 0)
+                load_scale_rows(nc, planes, w_scales, g // STRETCH)
+                w_planes.append(planes)
             w_tile = w_pool.tile([P, 2 * N_OUT], U8, align_bytes=64)
             nc.sync.dma_start(out=w_tile[:].bitcast(I32), in_=w_words[g])
             return w_tile
 
         w_tiles = [load_group(g) for g in range(W_BUFS)]
 
-        x_codes = keep.tile([P, GROUPS * TOKENS], U32, align_bytes=64)
-        x_planes = keep.tile([P, GROUPS * TOKENS], U8, align_bytes=64)
+        x_codes = []
+        x_planes = []
         for stretch in range(STRETCHES):
             x_words = x_chunks[stretch][:].bitcast(F32)
             grouped = grouped_pool.tile([P, STRETCH * TOKENS * PACK], BF16, align_bytes=64)
@@ -113,12 +116,11 @@ def tile_repro_pa_k_kernel(tc, hidden_states, w_qk_words, w_qk_scales, cos, sin,
                     out=grouped_words[:, 2 * bank : 2 * bank + 2, :, :],
                     in_=xt[:].rearrange("p g u r -> p g r u"),
                 )
-            columns = slice(stretch * STRETCH * TOKENS, (stretch + 1) * STRETCH * TOKENS)
-            nc.vector.quantize_mx(
-                out=x_codes[:, columns].bitcast(FP8X4),
-                scales=x_planes[:, columns],
-                in_=grouped[:],
-            )
+            codes = quantised_pool.tile([P, STRETCH * TOKENS], U32, align_bytes=64)
+            scales = quantised_pool.tile([P, STRETCH * TOKENS], U8, align_bytes=64)
+            nc.vector.quantize_mx(out=codes[:].bitcast(FP8X4), scales=scales[:], in_=grouped[:])
+            x_codes.append(codes)
+            x_planes.append(scales)
 
         cos_f = keep.tile([P, PAIRS], F32)
         sin_signed = keep.tile([P, 2, PAIRS], F32)
@@ -129,13 +131,14 @@ def tile_repro_pa_k_kernel(tc, hidden_states, w_qk_words, w_qk_scales, cos, sin,
         acc = [acc_pool.tile([P, N_TILE], F32, name="acc%d" % j) for j in range(BANKS)]
 
         def one_pass(g, j, w_codes):
-            tokens = slice(g * TOKENS, (g + 1) * TOKENS)
+            stretch, local = divmod(g, STRETCH)
+            tokens = slice(local * TOKENS, (local + 1) * TOKENS)
             nc.tensor.matmul_mx(
                 out=acc[j][:],
-                lhsT=x_codes[:, tokens].bitcast(FP8X4),
-                lhsT_scale=x_planes[:, tokens],
+                lhsT=x_codes[stretch][:, tokens].bitcast(FP8X4),
+                lhsT_scale=x_planes[stretch][:, tokens],
                 rhs=w_codes.bitcast(FP4X4),
-                rhs_scale=w_planes[:, g, j * N_TILE : (j + 1) * N_TILE],
+                rhs_scale=w_planes[stretch][:, local, j * N_TILE : (j + 1) * N_TILE],
                 start=(g == 0),
                 stop=(g == GROUPS - 1),
             )

@@ -27,7 +27,7 @@ GROUPS = FEATURES // K_PASS
 
 STRETCH = 8
 STRETCHES = GROUPS // STRETCH
-SCALE_GROUPS_PER_DMA = 4
+SCALE_GROUPS_PER_DMA = 32
 TAPER = 4
 MAIN_GROUPS = GROUPS - TAPER
 W_BUFS = 16
@@ -35,14 +35,13 @@ W_BUFS = 16
 FLOPS = 2 * TOKENS * FEATURES * N_OUT
 
 
-def load_scale_rows(nc, planes, w_scales, stretch):
-    for first in range(0, STRETCH, SCALE_GROUPS_PER_DMA):
-        local = slice(first, first + SCALE_GROUPS_PER_DMA)
-        groups = slice(stretch * STRETCH + first, stretch * STRETCH + first + SCALE_GROUPS_PER_DMA)
+def load_scale_rows(nc, w_planes, w_scales):
+    for first in range(0, GROUPS, SCALE_GROUPS_PER_DMA):
+        groups = slice(first, first + SCALE_GROUPS_PER_DMA)
         for quadrant in range(2):
             for row in range(4):
                 nc.sync.dma_start(
-                    out=planes[32 * quadrant + row : P : 64, local, :].bitcast(I32),
+                    out=w_planes[32 * quadrant + row : P : 64, groups, :].bitcast(I32),
                     in_=w_scales[groups, 4 * quadrant + row : 16 : 8, :].rearrange("g q n -> q g n"),
                 )
 
@@ -58,7 +57,6 @@ def tile_repro_pa_k_kernel(tc, hidden_states, w_qk_words, w_qk_scales, cos, sin,
         keep = stack.enter_context(tc.tile_pool(name="keep", bufs=1))
         x_pool = stack.enter_context(tc.tile_pool(name="x", bufs=STRETCHES))
         quantised_pool = stack.enter_context(tc.tile_pool(name="quantised", bufs=STRETCHES))
-        plane_pool = stack.enter_context(tc.tile_pool(name="planes", bufs=STRETCHES))
         grouped_pool = stack.enter_context(tc.tile_pool(name="grouped", bufs=2))
         w_pool = stack.enter_context(tc.tile_pool(name="w", bufs=W_BUFS))
         tail_pool = stack.enter_context(tc.tile_pool(name="tail", bufs=BANKS))
@@ -68,6 +66,9 @@ def tile_repro_pa_k_kernel(tc, hidden_states, w_qk_words, w_qk_scales, cos, sin,
 
         identity = keep.tile([P, P], F32)
         make_identity(nc, identity[:])
+
+        w_planes = keep.tile([P, GROUPS, N_OUT], U8, align_bytes=64)
+        nc.vector.memset(w_planes[:].bitcast(I32), 0)
 
         x_chunks = []
         for stretch in range(STRETCHES):
@@ -81,14 +82,9 @@ def tile_repro_pa_k_kernel(tc, hidden_states, w_qk_words, w_qk_scales, cos, sin,
             nc.sync.dma_start(out=cos_bf[b:P:BATCH, :], in_=cos)
             nc.sync.dma_start(out=sin_bf[b:P:BATCH, :], in_=sin)
 
-        w_planes = []
+        load_scale_rows(nc, w_planes, w_scales)
 
         def load_group(g):
-            if g % STRETCH == 0:
-                planes = plane_pool.tile([P, STRETCH, N_OUT], U8, align_bytes=64)
-                nc.vector.memset(planes[:].bitcast(I32), 0)
-                load_scale_rows(nc, planes, w_scales, g // STRETCH)
-                w_planes.append(planes)
             w_tile = w_pool.tile([P, 2 * N_OUT], U8, align_bytes=64)
             nc.sync.dma_start(out=w_tile[:].bitcast(I32), in_=w_words[g])
             return w_tile
@@ -138,7 +134,7 @@ def tile_repro_pa_k_kernel(tc, hidden_states, w_qk_words, w_qk_scales, cos, sin,
                 lhsT=x_codes[stretch][:, tokens].bitcast(FP8X4),
                 lhsT_scale=x_planes[stretch][:, tokens],
                 rhs=w_codes.bitcast(FP4X4),
-                rhs_scale=w_planes[stretch][:, local, j * N_TILE : (j + 1) * N_TILE],
+                rhs_scale=w_planes[:, g, j * N_TILE : (j + 1) * N_TILE],
                 start=(g == 0),
                 stop=(g == GROUPS - 1),
             )

@@ -27,21 +27,23 @@ GROUPS = FEATURES // K_PASS
 
 STRETCH = 8
 STRETCHES = GROUPS // STRETCH
-SCALE_GROUPS_PER_DMA = 32
+SCALE_GROUPS_PER_DMA = 4
 TAPER = 4
+TAPER_GROUPS_PER_DMA = 2
 MAIN_GROUPS = GROUPS - TAPER
-W_BUFS = 16
+W_BUFS = 12
 
 FLOPS = 2 * TOKENS * FEATURES * N_OUT
 
 
-def load_scale_rows(nc, w_planes, w_scales):
-    for first in range(0, GROUPS, SCALE_GROUPS_PER_DMA):
-        groups = slice(first, first + SCALE_GROUPS_PER_DMA)
+def load_scale_rows(nc, planes, w_scales, stretch):
+    for first in range(0, STRETCH, SCALE_GROUPS_PER_DMA):
+        local = slice(first, first + SCALE_GROUPS_PER_DMA)
+        groups = slice(stretch * STRETCH + first, stretch * STRETCH + first + SCALE_GROUPS_PER_DMA)
         for quadrant in range(2):
             for row in range(4):
                 nc.sync.dma_start(
-                    out=w_planes[32 * quadrant + row : P : 64, groups, :].bitcast(I32),
+                    out=planes[32 * quadrant + row : P : 64, local, :].bitcast(I32),
                     in_=w_scales[groups, 4 * quadrant + row : 16 : 8, :].rearrange("g q n -> q g n"),
                 )
 
@@ -57,18 +59,16 @@ def tile_repro_pa_k_kernel(tc, hidden_states, w_qk_words, w_qk_scales, cos, sin,
         keep = stack.enter_context(tc.tile_pool(name="keep", bufs=1))
         x_pool = stack.enter_context(tc.tile_pool(name="x", bufs=STRETCHES))
         quantised_pool = stack.enter_context(tc.tile_pool(name="quantised", bufs=STRETCHES))
+        plane_pool = stack.enter_context(tc.tile_pool(name="planes", bufs=STRETCHES))
         grouped_pool = stack.enter_context(tc.tile_pool(name="grouped", bufs=2))
         w_pool = stack.enter_context(tc.tile_pool(name="w", bufs=W_BUFS))
-        tail_pool = stack.enter_context(tc.tile_pool(name="tail", bufs=BANKS))
-        rope_pool = stack.enter_context(tc.tile_pool(name="rope", bufs=2))
+        tail_pool = stack.enter_context(tc.tile_pool(name="tail", bufs=BANKS * TAPER // TAPER_GROUPS_PER_DMA))
+        rope_pool = stack.enter_context(tc.tile_pool(name="rope", bufs=3))
         acc_pool = stack.enter_context(tc.psum_pool(name="acc", bufs=1))
         xt_pool = stack.enter_context(tc.psum_pool(name="xt", bufs=4))
 
         identity = keep.tile([P, P], F32)
         make_identity(nc, identity[:])
-
-        w_planes = keep.tile([P, GROUPS, N_OUT], U8, align_bytes=64)
-        nc.vector.memset(w_planes[:].bitcast(I32), 0)
 
         x_chunks = []
         for stretch in range(STRETCHES):
@@ -82,7 +82,12 @@ def tile_repro_pa_k_kernel(tc, hidden_states, w_qk_words, w_qk_scales, cos, sin,
             nc.sync.dma_start(out=cos_bf[b:P:BATCH, :], in_=cos)
             nc.sync.dma_start(out=sin_bf[b:P:BATCH, :], in_=sin)
 
-        load_scale_rows(nc, w_planes, w_scales)
+        w_planes = []
+        for stretch in range(STRETCHES):
+            planes = plane_pool.tile([P, STRETCH, N_OUT], U8, align_bytes=64)
+            nc.vector.memset(planes[:].bitcast(I32), 0)
+            load_scale_rows(nc, planes, w_scales, stretch)
+            w_planes.append(planes)
 
         def load_group(g):
             w_tile = w_pool.tile([P, 2 * N_OUT], U8, align_bytes=64)
@@ -134,7 +139,7 @@ def tile_repro_pa_k_kernel(tc, hidden_states, w_qk_words, w_qk_scales, cos, sin,
                 lhsT=x_codes[stretch][:, tokens].bitcast(FP8X4),
                 lhsT_scale=x_planes[stretch][:, tokens],
                 rhs=w_codes.bitcast(FP4X4),
-                rhs_scale=w_planes[:, g, j * N_TILE : (j + 1) * N_TILE],
+                rhs_scale=w_planes[stretch][:, local, j * N_TILE : (j + 1) * N_TILE],
                 start=(g == 0),
                 stop=(g == GROUPS - 1),
             )
@@ -145,18 +150,22 @@ def tile_repro_pa_k_kernel(tc, hidden_states, w_qk_words, w_qk_scales, cos, sin,
             if g + W_BUFS < MAIN_GROUPS:
                 w_tiles.append(load_group(g + W_BUFS))
 
-        tails = []
+        tails = {}
         for j in range(BANKS):
-            tail = tail_pool.tile([P, TAPER, 2 * N_TILE], U8, align_bytes=64)
-            nc.sync.dma_start(
-                out=tail[:].bitcast(I32),
-                in_=w_words[MAIN_GROUPS:GROUPS, :, j * N_TILE // 2 : (j + 1) * N_TILE // 2].rearrange("g p c -> p g c"),
-            )
-            tails.append(tail)
+            for first in range(MAIN_GROUPS, GROUPS, TAPER_GROUPS_PER_DMA):
+                tail = tail_pool.tile([P, TAPER_GROUPS_PER_DMA, 2 * N_TILE], U8, align_bytes=64)
+                nc.sync.dma_start(
+                    out=tail[:].bitcast(I32),
+                    in_=w_words[
+                        first : first + TAPER_GROUPS_PER_DMA, :, j * N_TILE // 2 : (j + 1) * N_TILE // 2
+                    ].rearrange("g p c -> p g c"),
+                )
+                for i in range(TAPER_GROUPS_PER_DMA):
+                    tails[(first + i, j)] = tail[:, i, :]
 
         for j in range(BANKS):
-            for i in range(TAPER):
-                one_pass(MAIN_GROUPS + i, j, tails[j][:, i, :])
+            for g in range(MAIN_GROUPS, GROUPS):
+                one_pass(g, j, tails[(g, j)])
 
             x = acc[j][:].rearrange("p (v r e) -> p v r e", r=PAIRS, e=2)
             by_cos = rope_pool.tile([P, VECTORS, PAIRS, 2], F32)
@@ -173,7 +182,8 @@ def tile_repro_pa_k_kernel(tc, hidden_states, w_qk_words, w_qk_scales, cos, sin,
                     in1=sin_signed[:, e, :].unsqueeze(1).to_broadcast([P, VECTORS, PAIRS]),
                 )
             rotated = rope_pool.tile([P, VECTORS, PAIRS, 2], F32)
-            nc.vector.tensor_add(
+            adder = nc.vector if j == BANKS - 1 else nc.gpsimd
+            adder.tensor_add(
                 out=rotated[:],
                 in0=by_cos[:],
                 in1=by_sin[:].rearrange("p e v r -> p v r e"),

@@ -27,7 +27,7 @@ GROUPS = FEATURES // K_PASS
 
 STRETCH = 8
 STRETCHES = GROUPS // STRETCH
-SCALE_GROUPS_PER_DMA = 4
+SCALE_GROUPS_PER_DMA = 8
 TAPER = 4
 TAPER_GROUPS_PER_DMA = 2
 MAIN_GROUPS = GROUPS - TAPER

@@ -27,7 +27,7 @@ GROUPS = FEATURES // K_PASS
 
 STRETCH = 8
 STRETCHES = GROUPS // STRETCH
-SCALE_GROUPS_PER_DMA = 8
+SCALE_GROUPS_PER_DMA = 4
 TAPER = 4
 TAPER_GROUPS_PER_DMA = 2
 MAIN_GROUPS = GROUPS - TAPER
@@ -76,18 +76,18 @@ def tile_repro_pa_k_kernel(tc, hidden_states, w_qk_words, w_qk_scales, cos, sin,
             columns = slice(stretch * STRETCH * K_PASS, (stretch + 1) * STRETCH * K_PASS)
             nc.sync.dma_start(out=x_chunk[:], in_=x_rows[:, columns])
             x_chunks.append(x_chunk)
-        cos_bf = keep.tile([P, PAIRS], BF16)
-        sin_bf = keep.tile([P, PAIRS], BF16)
-        for b in range(BATCH):
-            nc.sync.dma_start(out=cos_bf[b:P:BATCH, :], in_=cos)
-            nc.sync.dma_start(out=sin_bf[b:P:BATCH, :], in_=sin)
-
         w_planes = []
         for stretch in range(STRETCHES):
             planes = plane_pool.tile([P, STRETCH, N_OUT], U8, align_bytes=64)
             nc.vector.memset(planes[:].bitcast(I32), 0)
             load_scale_rows(nc, planes, w_scales, stretch)
             w_planes.append(planes)
+
+        cos_bf = keep.tile([P, PAIRS], BF16)
+        sin_bf = keep.tile([P, PAIRS], BF16)
+        for b in range(BATCH):
+            nc.sync.dma_start(out=cos_bf[b:P:BATCH, :], in_=cos)
+            nc.sync.dma_start(out=sin_bf[b:P:BATCH, :], in_=sin)
 
         def load_group(g):
             w_tile = w_pool.tile([P, 2 * N_OUT], U8, align_bytes=64)

@@ -27,7 +27,7 @@ GROUPS = FEATURES // K_PASS
 
 STRETCH = 8
 STRETCHES = GROUPS // STRETCH
-SCALE_GROUPS_PER_DMA = 4
+SCALE_GROUPS_PER_DMA = (8, 8, 8, 4)
 TAPER = 4
 TAPER_GROUPS_PER_DMA = 2
 MAIN_GROUPS = GROUPS - TAPER
@@ -37,9 +37,10 @@ FLOPS = 2 * TOKENS * FEATURES * N_OUT
 
 
 def load_scale_rows(nc, planes, w_scales, stretch):
-    for first in range(0, STRETCH, SCALE_GROUPS_PER_DMA):
-        local = slice(first, first + SCALE_GROUPS_PER_DMA)
-        groups = slice(stretch * STRETCH + first, stretch * STRETCH + first + SCALE_GROUPS_PER_DMA)
+    step = SCALE_GROUPS_PER_DMA[stretch]
+    for first in range(0, STRETCH, step):
+        local = slice(first, first + step)
+        groups = slice(stretch * STRETCH + first, stretch * STRETCH + first + step)
         for quadrant in range(2):
             for row in range(4):
                 nc.sync.dma_start(

@@ -27,7 +27,7 @@ GROUPS = FEATURES // K_PASS
 
 STRETCH = 8
 STRETCHES = GROUPS // STRETCH
-SCALE_GROUPS_PER_DMA = (8, 8, 8, 4)
+SCALE_SPANS = ((0, 24), (24, 28), (28, 32))
 TAPER = 4
 TAPER_GROUPS_PER_DMA = 2
 MAIN_GROUPS = GROUPS - TAPER
@@ -36,16 +36,13 @@ W_BUFS = 12
 FLOPS = 2 * TOKENS * FEATURES * N_OUT
 
 
-def load_scale_rows(nc, planes, w_scales, stretch):
-    step = SCALE_GROUPS_PER_DMA[stretch]
-    for first in range(0, STRETCH, step):
-        local = slice(first, first + step)
-        groups = slice(stretch * STRETCH + first, stretch * STRETCH + first + step)
+def load_scale_rows(nc, planes, w_scales):
+    for first, end in SCALE_SPANS:
         for quadrant in range(2):
             for row in range(4):
                 nc.sync.dma_start(
-                    out=planes[32 * quadrant + row : P : 64, local, :].bitcast(I32),
-                    in_=w_scales[groups, 4 * quadrant + row : 16 : 8, :].rearrange("g q n -> q g n"),
+                    out=planes[32 * quadrant + row : P : 64, first:end, :].bitcast(I32),
+                    in_=w_scales[first:end, 4 * quadrant + row : 16 : 8, :].rearrange("g q n -> q g n"),
                 )
 
 
@@ -60,7 +57,6 @@ def tile_repro_pa_k_kernel(tc, hidden_states, w_qk_words, w_qk_scales, cos, sin,
         keep = stack.enter_context(tc.tile_pool(name="keep", bufs=1))
         x_pool = stack.enter_context(tc.tile_pool(name="x", bufs=STRETCHES))
         quantised_pool = stack.enter_context(tc.tile_pool(name="quantised", bufs=STRETCHES))
-        plane_pool = stack.enter_context(tc.tile_pool(name="planes", bufs=STRETCHES))
         grouped_pool = stack.enter_context(tc.tile_pool(name="grouped", bufs=2))
         w_pool = stack.enter_context(tc.tile_pool(name="w", bufs=W_BUFS))
         tail_pool = stack.enter_context(tc.tile_pool(name="tail", bufs=BANKS * TAPER // TAPER_GROUPS_PER_DMA))
@@ -77,12 +73,10 @@ def tile_repro_pa_k_kernel(tc, hidden_states, w_qk_words, w_qk_scales, cos, sin,
             columns = slice(stretch * STRETCH * K_PASS, (stretch + 1) * STRETCH * K_PASS)
             nc.sync.dma_start(out=x_chunk[:], in_=x_rows[:, columns])
             x_chunks.append(x_chunk)
-        w_planes = []
+        w_planes = keep.tile([P, GROUPS, N_OUT], U8, align_bytes=64)
         for stretch in range(STRETCHES):
-            planes = plane_pool.tile([P, STRETCH, N_OUT], U8, align_bytes=64)
-            nc.vector.memset(planes[:].bitcast(I32), 0)
-            load_scale_rows(nc, planes, w_scales, stretch)
-            w_planes.append(planes)
+            nc.vector.memset(w_planes[:, stretch * STRETCH : (stretch + 1) * STRETCH, :].bitcast(I32), 0)
+        load_scale_rows(nc, w_planes, w_scales)
 
         cos_bf = keep.tile([P, PAIRS], BF16)
         sin_bf = keep.tile([P, PAIRS], BF16)
@@ -140,7 +134,7 @@ def tile_repro_pa_k_kernel(tc, hidden_states, w_qk_words, w_qk_scales, cos, sin,
                 lhsT=x_codes[stretch][:, tokens].bitcast(FP8X4),
                 lhsT_scale=x_planes[stretch][:, tokens],
                 rhs=w_codes.bitcast(FP4X4),
-                rhs_scale=w_planes[stretch][:, local, j * N_TILE : (j + 1) * N_TILE],
+                rhs_scale=w_planes[:, g, j * N_TILE : (j + 1) * N_TILE],
                 start=(g == 0),
                 stop=(g == GROUPS - 1),
             )

@@ -162,33 +162,39 @@ def tile_repro_pa_k_kernel(tc, hidden_states, w_qk_words, w_qk_scales, cos, sin,
             for g in range(MAIN_GROUPS, GROUPS):
                 one_pass(g, j, tails[(g, j)])
 
-            x = acc[j][:].rearrange("p (v r e) -> p v r e", r=PAIRS, e=2)
-            by_cos = rope_pool.tile([P, VECTORS, PAIRS, 2], F32)
-            nc.vector.tensor_mul(
-                out=by_cos[:],
-                in0=x,
-                in1=cos_f[:].unsqueeze(1).unsqueeze(3).to_broadcast([P, VECTORS, PAIRS, 2]),
-            )
-            by_sin = rope_pool.tile([P, 2, VECTORS, PAIRS], F32)
-            for e in range(2):
+            if j < BANKS - 1:
+                parts = ((0, HEADS_PER_BANK, nc.gpsimd),)
+            else:
+                parts = ((0, HEADS_PER_BANK // 2, nc.gpsimd), (HEADS_PER_BANK // 2, HEADS_PER_BANK // 2, nc.vector))
+            for head0, heads, adder in parts:
+                vectors = 2 * heads
+                columns = slice(head0 * 2 * HEAD_DIM, (head0 + heads) * 2 * HEAD_DIM)
+                x = acc[j][:, columns].rearrange("p (v r e) -> p v r e", r=PAIRS, e=2)
+                by_cos = rope_pool.tile([P, vectors, PAIRS, 2], F32)
                 nc.vector.tensor_mul(
-                    out=by_sin[:, e, :, :],
-                    in0=x[:, :, :, 1 - e],
-                    in1=sin_signed[:, e, :].unsqueeze(1).to_broadcast([P, VECTORS, PAIRS]),
+                    out=by_cos[:],
+                    in0=x,
+                    in1=cos_f[:].unsqueeze(1).unsqueeze(3).to_broadcast([P, vectors, PAIRS, 2]),
                 )
-            rotated = rope_pool.tile([P, VECTORS, PAIRS, 2], F32)
-            adder = nc.vector if j == BANKS - 1 else nc.gpsimd
-            adder.tensor_add(
-                out=rotated[:],
-                in0=by_cos[:],
-                in1=by_sin[:].rearrange("p e v r -> p v r e"),
-            )
-
-            by_head = rotated[:].rearrange("p (h t) r e -> p h t (r e)", t=2)
-            for t, out_t in enumerate((out_0, out_1)):
-                for b in range(BATCH):
-                    first_head = b * HEADS + j * HEADS_PER_BANK
-                    nc.sync.dma_start(
-                        out=out_t[first_head : first_head + HEADS_PER_BANK].rearrange("h s d -> s h d"),
-                        in_=by_head[b:P:BATCH, :, t, :],
+                by_sin = rope_pool.tile([P, 2, vectors, PAIRS], F32)
+                for e in range(2):
+                    nc.vector.tensor_mul(
+                        out=by_sin[:, e, :, :],
+                        in0=x[:, :, :, 1 - e],
+                        in1=sin_signed[:, e, :].unsqueeze(1).to_broadcast([P, vectors, PAIRS]),
                     )
+                rotated = rope_pool.tile([P, vectors, PAIRS, 2], F32)
+                adder.tensor_add(
+                    out=rotated[:],
+                    in0=by_cos[:],
+                    in1=by_sin[:].rearrange("p e v r -> p v r e"),
+                )
+
+                by_head = rotated[:].rearrange("p (h t) r e -> p h t (r e)", t=2)
+                for t, out_t in enumerate((out_0, out_1)):
+                    for b in range(BATCH):
+                        first_head = b * HEADS + j * HEADS_PER_BANK + head0
+                        nc.sync.dma_start(
+                            out=out_t[first_head : first_head + heads].rearrange("h s d -> s h d"),
+                            in_=by_head[b:P:BATCH, :, t, :],
+                        )

@@ -40,9 +40,13 @@ def load_scale_rows(nc, planes, w_scales):
     for first, end in SCALE_SPANS:
         for quadrant in range(2):
             for row in range(4):
-                nc.sync.dma_start(
-                    out=planes[32 * quadrant + row : P : 64, first:end, :].bitcast(I32),
-                    in_=w_scales[first:end, 4 * quadrant + row : 16 : 8, :].rearrange("g q n -> q g n"),
+                if end - first > STRETCH and row % 2 == 1:
+                    queue, words = nc.scalar, F32
+                else:
+                    queue, words = nc.sync, I32
+                queue.dma_start(
+                    out=planes[32 * quadrant + row : P : 64, first:end, :].bitcast(words),
+                    in_=w_scales[first:end, 4 * quadrant + row : 16 : 8, :].bitcast(words).rearrange("g q n -> q g n"),
                 )
 
 
@@ -50,7 +54,7 @@ def tile_repro_pa_k_kernel(tc, hidden_states, w_qk_words, w_qk_scales, cos, sin,
     nc = tc.nc
     x_rows = hidden_states.rearrange("s b k -> (s b) k")
     w_words = w_qk_words.bitcast(I32)
-    w_scales = w_qk_scales.bitcast(I32)
+    w_scales = w_qk_scales
 
     with ExitStack() as stack:
         stack.enter_context(tc.manual_schedule())

from contextlib import ExitStack

import concourse.mybir as mybir
from concourse.masks import make_identity

F32 = mybir.dt.float32
BF16 = mybir.dt.bfloat16
I32 = mybir.dt.int32
U32 = mybir.dt.uint32
U8 = mybir.dt.uint8
FP8X4 = mybir.dt.float8_e4m3fn_x4
FP4X4 = mybir.dt.float4_e2m1fn_x4

P = 128
PACK = 4
K_PASS = P * PACK
POSITIONS, BATCH, FEATURES = 64, 2, 16384
TOKENS = POSITIONS * BATCH
HEADS, HEAD_DIM = 16, 64
PAIRS = HEAD_DIM // 2
N_OUT = HEADS * 2 * HEAD_DIM
N_TILE = 512
BANKS = N_OUT // N_TILE
VECTORS = N_TILE // HEAD_DIM
HEADS_PER_BANK = VECTORS // 2
GROUPS = FEATURES // K_PASS

STRETCH = 8
STRETCHES = GROUPS // STRETCH
SCALE_SPANS = ((0, 24), (24, 28), (28, 32))
TAPER = 4
TAPER_GROUPS_PER_DMA = 2
MAIN_GROUPS = GROUPS - TAPER
W_BUFS = 12

FLOPS = 2 * TOKENS * FEATURES * N_OUT


def load_scale_rows(nc, planes, w_scales):
    for first, end in SCALE_SPANS:
        for quadrant in range(2):
            for row in range(4):
                if end - first > STRETCH and row % 2 == 1:
                    queue, words = nc.scalar, F32
                else:
                    queue, words = nc.sync, I32
                queue.dma_start(
                    out=planes[32 * quadrant + row : P : 64, first:end, :].bitcast(words),
                    in_=w_scales[first:end, 4 * quadrant + row : 16 : 8, :].bitcast(words).rearrange("g q n -> q g n"),
                )


def tile_repro_pa_k_kernel(tc, hidden_states, w_qk_words, w_qk_scales, cos, sin, out_0, out_1):
    nc = tc.nc
    x_rows = hidden_states.rearrange("s b k -> (s b) k")
    w_words = w_qk_words.bitcast(I32)
    w_scales = w_qk_scales

    with ExitStack() as stack:
        stack.enter_context(tc.manual_schedule())
        keep = stack.enter_context(tc.tile_pool(name="keep", bufs=1))
        x_pool = stack.enter_context(tc.tile_pool(name="x", bufs=STRETCHES))
        quantised_pool = stack.enter_context(tc.tile_pool(name="quantised", bufs=STRETCHES))
        grouped_pool = stack.enter_context(tc.tile_pool(name="grouped", bufs=2))
        w_pool = stack.enter_context(tc.tile_pool(name="w", bufs=W_BUFS))
        tail_pool = stack.enter_context(tc.tile_pool(name="tail", bufs=BANKS * TAPER // TAPER_GROUPS_PER_DMA))
        rope_pool = stack.enter_context(tc.tile_pool(name="rope", bufs=3))
        acc_pool = stack.enter_context(tc.psum_pool(name="acc", bufs=1))
        xt_pool = stack.enter_context(tc.psum_pool(name="xt", bufs=4))

        identity = keep.tile([P, P], F32)
        make_identity(nc, identity[:])

        x_chunks = []
        for stretch in range(STRETCHES):
            x_chunk = x_pool.tile([P, STRETCH * K_PASS], BF16)
            columns = slice(stretch * STRETCH * K_PASS, (stretch + 1) * STRETCH * K_PASS)
            nc.sync.dma_start(out=x_chunk[:], in_=x_rows[:, columns])
            x_chunks.append(x_chunk)
        w_planes = keep.tile([P, GROUPS, N_OUT], U8, align_bytes=64)
        for stretch in range(STRETCHES):
            nc.vector.memset(w_planes[:, stretch * STRETCH : (stretch + 1) * STRETCH, :].bitcast(I32), 0)
        load_scale_rows(nc, w_planes, w_scales)

        cos_bf = keep.tile([P, PAIRS], BF16)
        sin_bf = keep.tile([P, PAIRS], BF16)
        for b in range(BATCH):
            nc.sync.dma_start(out=cos_bf[b:P:BATCH, :], in_=cos)
            nc.sync.dma_start(out=sin_bf[b:P:BATCH, :], in_=sin)

        def load_group(g):
            w_tile = w_pool.tile([P, 2 * N_OUT], U8, align_bytes=64)
            nc.sync.dma_start(out=w_tile[:].bitcast(I32), in_=w_words[g])
            return w_tile

        w_tiles = [load_group(g) for g in range(W_BUFS)]

        x_codes = []
        x_planes = []
        for stretch in range(STRETCHES):
            x_words = x_chunks[stretch][:].bitcast(F32)
            grouped = grouped_pool.tile([P, STRETCH * TOKENS * PACK], BF16, align_bytes=64)
            grouped_words = grouped[:].bitcast(F32).rearrange("p (g r u) -> p g r u", g=STRETCH, u=2)
            for bank in range(STRETCH // 2):
                xt = xt_pool.tile([P, 2, 2, TOKENS], F32)
                for i in range(2):
                    g = 2 * bank + i
                    for u in range(2):
                        nc.tensor.transpose(
                            out=xt[:, i, u, :],
                            in_=x_words[:, 256 * g + u : 256 * (g + 1) : 2],
                            identity=identity[:],
                        )
                copy_out = nc.vector.tensor_copy if bank % 2 == 0 else nc.scalar.copy
                copy_out(
                    out=grouped_words[:, 2 * bank : 2 * bank + 2, :, :],
                    in_=xt[:].rearrange("p g u r -> p g r u"),
                )
            codes = quantised_pool.tile([P, STRETCH * TOKENS], U32, align_bytes=64)
            scales = quantised_pool.tile([P, STRETCH * TOKENS], U8, align_bytes=64)
            nc.vector.quantize_mx(out=codes[:].bitcast(FP8X4), scales=scales[:], in_=grouped[:])
            x_codes.append(codes)
            x_planes.append(scales)

        cos_f = keep.tile([P, PAIRS], F32)
        sin_signed = keep.tile([P, 2, PAIRS], F32)
        nc.vector.tensor_copy(out=cos_f[:], in_=cos_bf[:])
        nc.vector.tensor_scalar_mul(out=sin_signed[:, 0, :], in0=sin_bf[:], scalar1=-1.0)
        nc.vector.tensor_copy(out=sin_signed[:, 1, :], in_=sin_bf[:])

        acc = [acc_pool.tile([P, N_TILE], F32, name="acc%d" % j) for j in range(BANKS)]

        def one_pass(g, j, w_codes):
            stretch, local = divmod(g, STRETCH)
            tokens = slice(local * TOKENS, (local + 1) * TOKENS)
            nc.tensor.matmul_mx(
                out=acc[j][:],
                lhsT=x_codes[stretch][:, tokens].bitcast(FP8X4),
                lhsT_scale=x_planes[stretch][:, tokens],
                rhs=w_codes.bitcast(FP4X4),
                rhs_scale=w_planes[:, g, j * N_TILE : (j + 1) * N_TILE],
                start=(g == 0),
                stop=(g == GROUPS - 1),
            )

        for g in range(MAIN_GROUPS):
            for j in range(BANKS):
                one_pass(g, j, w_tiles[g][:, 2 * j * N_TILE : 2 * (j + 1) * N_TILE])
            if g + W_BUFS < MAIN_GROUPS:
                w_tiles.append(load_group(g + W_BUFS))

        tails = {}
        for j in range(BANKS):
            for first in range(MAIN_GROUPS, GROUPS, TAPER_GROUPS_PER_DMA):
                tail = tail_pool.tile([P, TAPER_GROUPS_PER_DMA, 2 * N_TILE], U8, align_bytes=64)
                nc.sync.dma_start(
                    out=tail[:].bitcast(I32),
                    in_=w_words[
                        first : first + TAPER_GROUPS_PER_DMA, :, j * N_TILE // 2 : (j + 1) * N_TILE // 2
                    ].rearrange("g p c -> p g c"),
                )
                for i in range(TAPER_GROUPS_PER_DMA):
                    tails[(first + i, j)] = tail[:, i, :]

        for j in range(BANKS):
            for g in range(MAIN_GROUPS, GROUPS):
                one_pass(g, j, tails[(g, j)])

            if j < BANKS - 1:
                parts = ((0, HEADS_PER_BANK, nc.gpsimd),)
            else:
                parts = ((0, HEADS_PER_BANK // 2, nc.gpsimd), (HEADS_PER_BANK // 2, HEADS_PER_BANK // 2, nc.vector))
            for head0, heads, adder in parts:
                vectors = 2 * heads
                columns = slice(head0 * 2 * HEAD_DIM, (head0 + heads) * 2 * HEAD_DIM)
                x = acc[j][:, columns].rearrange("p (v r e) -> p v r e", r=PAIRS, e=2)
                by_cos = rope_pool.tile([P, vectors, PAIRS, 2], F32)
                nc.vector.tensor_mul(
                    out=by_cos[:],
                    in0=x,
                    in1=cos_f[:].unsqueeze(1).unsqueeze(3).to_broadcast([P, vectors, PAIRS, 2]),
                )
                by_sin = rope_pool.tile([P, 2, vectors, PAIRS], F32)
                for e in range(2):
                    nc.vector.tensor_mul(
                        out=by_sin[:, e, :, :],
                        in0=x[:, :, :, 1 - e],
                        in1=sin_signed[:, e, :].unsqueeze(1).to_broadcast([P, vectors, PAIRS]),
                    )
                rotated = rope_pool.tile([P, vectors, PAIRS, 2], F32)
                adder.tensor_add(
                    out=rotated[:],
                    in0=by_cos[:],
                    in1=by_sin[:].rearrange("p e v r -> p v r e"),
                )

                by_head = rotated[:].rearrange("p (h t) r e -> p h t (r e)", t=2)
                for t, out_t in enumerate((out_0, out_1)):
                    for b in range(BATCH):
                        first_head = b * HEADS + j * HEADS_PER_BANK + head0
                        nc.sync.dma_start(
                            out=out_t[first_head : first_head + heads].rearrange("h s d -> s h d"),
                            in_=by_head[b:P:BATCH, :, t, :],
                        )
